import numpy as np
import ml_dtypes


def mxq(x, axis, fmt="e4m3"):
    dtype, down = {"e4m3": (ml_dtypes.float8_e4m3fn, 7), "e5m2": (ml_dtypes.float8_e5m2, 14)}[fmt]
    v = np.moveaxis(np.asarray(x, np.float32).astype(ml_dtypes.bfloat16).astype(np.float64), axis, -1)
    blocks = v.reshape(v.shape[:-1] + (-1, 32))
    amax = np.abs(blocks).max(-1, keepdims=True)
    byte = np.maximum(np.where(amax > 0, np.frexp(amax)[1] - 1 + 127, 0) - down, 1)
    scale = np.exp2(byte - 127.0)
    codes = (blocks / scale).astype(np.float32).astype(dtype).astype(np.float64)
    return np.moveaxis((codes * scale).reshape(v.shape), -1, axis)


WIDE = False


def mx_kscale(k):
    if not WIDE:
        return np.ones(k)
    levels = np.array([20, -20, 10, -10, 0])
    a = np.random.permutation(np.resize(levels, k // 512 * 4)).reshape(k // 512, 4)
    idx = np.arange(k)
    return np.exp2(a[idx // 512, idx % 128 // 32])


BF16 = ml_dtypes.bfloat16


def bf(x):
    return np.asarray(x, np.float32).astype(BF16)


def f64(x):
    return np.asarray(x).astype(np.float64)


B, M, F, U = 1024, 4, 512, 512


def setup_inputs():
    u = mx_kscale(U)
    limit = np.sqrt(6.0 / (F + U))
    x = bf(np.random.standard_normal((B, M, F)))
    W0 = bf(np.random.uniform(-limit, limit, (M, F, U)))
    b = bf(np.random.standard_normal((M, U)) * 0.1)
    g = bf(np.random.standard_normal((B, M * U)) * np.exp2(np.random.randint(-12, 1, (B, 1))) * 64.0 * np.tile(u, M)[None, :])
    z = (f64(x).transpose(1, 0, 2) @ f64(W0)).transpose(1, 0, 2) + f64(b)[None, :, :]
    return {"x": x, "W": bf(f64(W0) / u[None, None, :]), "b": b,
            "z": np.asarray(z, np.float32), "grad_out": g}


def reference(x, W, b, z, grad_out):
    g = f64(grad_out).reshape(B, M, U)
    dz = np.where(f64(z) > 0.0, g, 0.0)
    dq = mxq(dz, 2, "e5m2")
    wq = mxq(f64(W), 2, "e4m3")
    gx = dq.transpose(1, 0, 2) @ wq.transpose(0, 2, 1)
    return gx.transpose(1, 0, 2)

@@ -1,0 +1,159 @@
+from contextlib import ExitStack
+
+import concourse.mybir as mybir
+from concourse.masks import make_identity
+
+F32 = mybir.dt.float32
+BF16 = mybir.dt.bfloat16
+U32 = mybir.dt.uint32
+U8 = mybir.dt.uint8
+E5M2_X4 = mybir.dt.float8_e5m2_x4
+E4M3_X4 = mybir.dt.float8_e4m3fn_x4
+ALU = mybir.AluOpType
+
+P = 128
+PACK = 4
+TOKENS, MASKS, K, F = 1024, 4, 512, 512
+TILES = TOKENS // P
+ROW = MASKS * K
+W_ROWS = F // P
+HALVES = 2
+WORDS = K // 2
+BANK_BLOCKS = 2
+G_TILES = 2
+OUT_TILES = 2
+
+FLOPS = 2 * TOKENS * MASKS * K * F
+BYTES = 2 * MASKS * F * K + 4 * TOKENS * ROW + 2 * TOKENS * ROW + 4 * TOKENS * ROW
+
+
+def transpose_bank(nc, psum_t, identity, words, bank_index):
+    bank = psum_t.tile([P, BANK_BLOCKS, HALVES, P], F32)
+    first = bank_index * BANK_BLOCKS * WORDS
+    for b in range(BANK_BLOCKS):
+        for u in range(HALVES):
+            start = first + (b * HALVES + u) * P
+            nc.tensor.transpose(
+                out=bank[:, b, u, :], in_=words[:, start : start + P], identity=identity
+            )
+    return bank
+
+
+def tile_paralleldense_t_v_kernel(tc, x, W, b, z, grad_out, out):
+    nc = tc.nc
+    with ExitStack() as ctx:
+        const = ctx.enter_context(tc.tile_pool(name="const", bufs=1))
+        w_in = ctx.enter_context(tc.tile_pool(name="w_in", bufs=MASKS))
+        g_in = ctx.enter_context(tc.tile_pool(name="g_in", bufs=TILES // G_TILES))
+        z_in = ctx.enter_context(tc.tile_pool(name="z_in", bufs=TILES))
+        result = ctx.enter_context(tc.tile_pool(name="result", bufs=TILES // OUT_TILES))
+        masked = ctx.enter_context(tc.tile_pool(name="masked", bufs=2))
+        regroup = ctx.enter_context(tc.tile_pool(name="regroup", bufs=3))
+        dz_mx = ctx.enter_context(tc.tile_pool(name="dz_mx", bufs=2))
+        psum_t = ctx.enter_context(tc.psum_pool(name="psum_t", bufs=4))
+        psum_o = ctx.enter_context(tc.psum_pool(name="psum_o", bufs=4))
+
+        w_rows = []
+        for m in range(MASKS):
+            w_sb = w_in.tile([P, W_ROWS * K], BF16)
+            nc.sync.dma_start(
+                out=w_sb[:], in_=W[m].rearrange("(p c) k -> p (c k)", c=W_ROWS)
+            )
+            w_rows.append(w_sb)
+
+        g_view = grad_out.rearrange("(p t) c -> p t c", t=TILES)
+        z_view = z.rearrange("(p t) m k -> p t (m k)", t=TILES)
+        out_view = out.rearrange("(p t) m f -> p t (m f)", t=TILES)
+        g_tiles = []
+        z_tiles = []
+        for t in range(TILES):
+            if t % G_TILES == 0:
+                g_sb = g_in.tile([P, G_TILES, ROW], BF16)
+                nc.sync.dma_start(out=g_sb[:], in_=g_view[:, t : t + G_TILES, :])
+                g_tiles.append(g_sb)
+            z_sb = z_in.tile([P, ROW], F32)
+            nc.sync.dma_start(out=z_sb[:], in_=z_view[:, t, :])
+            z_tiles.append(z_sb)
+
+        identity = const.tile([P, P], F32)
+        make_identity(nc, identity[:])
+
+        w_codes = const.tile([P, MASKS, F], U32, align_bytes=64)
+        w_scales = const.tile([P, MASKS, F], U8, align_bytes=64)
+        for m in range(MASKS):
+            w_grouped = regroup.tile([P, F * PACK], BF16, tag="grouped", align_bytes=64)
+            w_grouped_words = (
+                w_grouped[:]
+                .bitcast(F32)
+                .rearrange("w (p c u) -> w p c u", c=W_ROWS, u=HALVES)
+            )
+            for h in range(W_ROWS // BANK_BLOCKS):
+                bank = transpose_bank(nc, psum_t, identity[:], w_rows[m][:].bitcast(F32), h)
+                nc.scalar.copy(
+                    out=w_grouped_words[:, :, h * BANK_BLOCKS : (h + 1) * BANK_BLOCKS, :],
+                    in_=bank[:].rearrange("w c u p -> w p c u"),
+                )
+            nc.vector.quantize_mx(
+                out=w_codes[:, m, :].bitcast(E4M3_X4),
+                scales=w_scales[:, m, :],
+                in_=w_grouped[:],
+            )
+
+        def mask_and_transpose(t):
+            dz = masked.tile([P, ROW], BF16)
+            nc.vector.scalar_tensor_tensor(
+                out=dz[:],
+                in0=z_tiles[t][:],
+                scalar=0.0,
+                in1=g_tiles[t // G_TILES][:, t % G_TILES, :],
+                op0=ALU.is_gt,
+                op1=ALU.mult,
+            )
+            dz_grouped = regroup.tile([P, MASKS * P * PACK], BF16, tag="grouped", align_bytes=64)
+            dz_grouped_words = (
+                dz_grouped[:]
+                .bitcast(F32)
+                .rearrange("w (m i u) -> w m i u", m=MASKS, u=HALVES)
+            )
+            for h in range(MASKS // BANK_BLOCKS):
+                bank = transpose_bank(nc, psum_t, identity[:], dz[:].bitcast(F32), h)
+                nc.scalar.copy(
+                    out=dz_grouped_words[:, h * BANK_BLOCKS : (h + 1) * BANK_BLOCKS, :, :],
+                    in_=bank[:].rearrange("w m u i -> w m i u"),
+                )
+            return dz_grouped
+
+        def quantise_and_multiply(t, dz_grouped, out_sb):
+            dz_codes = dz_mx.tile([P, MASKS * P], U32, align_bytes=64)
+            dz_scales = dz_mx.tile([P, MASKS * P], U8, align_bytes=64)
+            nc.vector.quantize_mx(
+                out=dz_codes[:].bitcast(E5M2_X4), scales=dz_scales[:], in_=dz_grouped[:]
+            )
+            for m in range(MASKS):
+                tokens = slice(m * P, (m + 1) * P)
+                acc = psum_o.tile([P, F], F32)
+                nc.tensor.matmul_mx(
+                    out=acc[:],
+                    lhsT=dz_codes[:, tokens].bitcast(E5M2_X4),
+                    lhsT_scale=dz_scales[:, tokens],
+                    rhs=w_codes[:, m, :].bitcast(E4M3_X4),
+                    rhs_scale=w_scales[:, m, :],
+                    start=True,
+                    stop=True,
+                )
+                nc.scalar.copy(
+                    out=out_sb[:, t % OUT_TILES, m * F : (m + 1) * F], in_=acc[:]
+                )
+
+        grouped_next = mask_and_transpose(0)
+        for t in range(TILES):
+            grouped_now = grouped_next
+            if t + 1 < TILES:
+                grouped_next = mask_and_transpose(t + 1)
+            if t % OUT_TILES == 0:
+                out_sb = result.tile([P, OUT_TILES, ROW], F32)
+            quantise_and_multiply(t, grouped_now, out_sb)
+            if t % OUT_TILES == OUT_TILES - 1:
+                nc.sync.dma_start(
+                    out=out_view[:, t + 1 - OUT_TILES : t + 1, :], in_=out_sb[:]
+                )

@@ -21,7 +21,8 @@ HALVES = 2
 WORDS = K // 2
 BANK_BLOCKS = 2
 G_TILES = 2
-OUT_TILES = 2
+OUT_TILES = 1
+VECTOR_MASK = MASKS - 1
 
 FLOPS = 2 * TOKENS * MASKS * K * F
 BYTES = 2 * MASKS * F * K + 4 * TOKENS * ROW + 2 * TOKENS * ROW + 4 * TOKENS * ROW
@@ -141,9 +142,11 @@ def tile_paralleldense_t_v_kernel(tc, x, W, b, z, grad_out, out):
                     start=True,
                     stop=True,
                 )
-                nc.scalar.copy(
-                    out=out_sb[:, t % OUT_TILES, m * F : (m + 1) * F], in_=acc[:]
-                )
+                out_cols = out_sb[:, t % OUT_TILES, m * F : (m + 1) * F]
+                if m == VECTOR_MASK:
+                    nc.vector.tensor_copy(out=out_cols, in_=acc[:])
+                else:
+                    nc.scalar.copy(out=out_cols, in_=acc[:])
 
         grouped_next = mask_and_transpose(0)
         for t in range(TILES):

@@ -16,12 +16,13 @@ PACK = 4
 TOKENS, MASKS, K, F = 1024, 4, 512, 512
 TILES = TOKENS // P
 ROW = MASKS * K
-W_ROWS = F // P
+W_ROWS = MASKS * F // P
 HALVES = 2
 WORDS = K // 2
 BANK_BLOCKS = 2
-G_TILES = 2
-OUT_TILES = 1
+G_TILES = 4
+Z_TILES = 2
+STORE_TILES = (4, 2, 2)
 VECTOR_MASK = MASKS - 1
 
 FLOPS = 2 * TOKENS * MASKS * K * F
@@ -44,23 +45,18 @@ def tile_paralleldense_t_v_kernel(tc, x, W, b, z, grad_out, out):
     nc = tc.nc
     with ExitStack() as ctx:
         const = ctx.enter_context(tc.tile_pool(name="const", bufs=1))
-        w_in = ctx.enter_context(tc.tile_pool(name="w_in", bufs=MASKS))
+        w_in = ctx.enter_context(tc.tile_pool(name="w_in", bufs=1))
         g_in = ctx.enter_context(tc.tile_pool(name="g_in", bufs=TILES // G_TILES))
-        z_in = ctx.enter_context(tc.tile_pool(name="z_in", bufs=TILES))
-        result = ctx.enter_context(tc.tile_pool(name="result", bufs=TILES // OUT_TILES))
+        z_in = ctx.enter_context(tc.tile_pool(name="z_in", bufs=TILES // Z_TILES))
+        result = ctx.enter_context(tc.tile_pool(name="result", bufs=1))
         masked = ctx.enter_context(tc.tile_pool(name="masked", bufs=2))
         regroup = ctx.enter_context(tc.tile_pool(name="regroup", bufs=3))
         dz_mx = ctx.enter_context(tc.tile_pool(name="dz_mx", bufs=2))
         psum_t = ctx.enter_context(tc.psum_pool(name="psum_t", bufs=4))
         psum_o = ctx.enter_context(tc.psum_pool(name="psum_o", bufs=4))
 
-        w_rows = []
-        for m in range(MASKS):
-            w_sb = w_in.tile([P, W_ROWS * K], BF16)
-            nc.sync.dma_start(
-                out=w_sb[:], in_=W[m].rearrange("(p c) k -> p (c k)", c=W_ROWS)
-            )
-            w_rows.append(w_sb)
+        w_sb = w_in.tile([P, W_ROWS * K], BF16)
+        nc.sync.dma_start(out=w_sb[:], in_=W.rearrange("m (q c) k -> (m q) (c k)", c=W_ROWS))
 
         g_view = grad_out.rearrange("(p t) c -> p t c", t=TILES)
         z_view = z.rearrange("(p t) m k -> p t (m k)", t=TILES)
@@ -72,39 +68,38 @@ def tile_paralleldense_t_v_kernel(tc, x, W, b, z, grad_out, out):
                 g_sb = g_in.tile([P, G_TILES, ROW], BF16)
                 nc.sync.dma_start(out=g_sb[:], in_=g_view[:, t : t + G_TILES, :])
                 g_tiles.append(g_sb)
-            z_sb = z_in.tile([P, ROW], F32)
-            nc.sync.dma_start(out=z_sb[:], in_=z_view[:, t, :])
-            z_tiles.append(z_sb)
+            if t % Z_TILES == 0:
+                z_sb = z_in.tile([P, Z_TILES, ROW], F32)
+                nc.sync.dma_start(out=z_sb[:], in_=z_view[:, t : t + Z_TILES, :])
+                z_tiles.append(z_sb)
 
         identity = const.tile([P, P], F32)
         make_identity(nc, identity[:])
 
         w_codes = const.tile([P, MASKS, F], U32, align_bytes=64)
         w_scales = const.tile([P, MASKS, F], U8, align_bytes=64)
-        for m in range(MASKS):
-            w_grouped = regroup.tile([P, F * PACK], BF16, tag="grouped", align_bytes=64)
-            w_grouped_words = (
-                w_grouped[:]
-                .bitcast(F32)
-                .rearrange("w (p c u) -> w p c u", c=W_ROWS, u=HALVES)
+        w_grouped = const.tile([P, MASKS * F * PACK], BF16, align_bytes=64)
+        w_grouped_words = (
+            w_grouped[:].bitcast(F32).rearrange("w (p c u) -> w p c u", c=W_ROWS, u=HALVES)
+        )
+        for h in range(W_ROWS // BANK_BLOCKS):
+            bank = transpose_bank(nc, psum_t, identity[:], w_sb[:].bitcast(F32), h)
+            nc.scalar.copy(
+                out=w_grouped_words[:, :, h * BANK_BLOCKS : (h + 1) * BANK_BLOCKS, :],
+                in_=bank[:].rearrange("w c u p -> w p c u"),
             )
-            for h in range(W_ROWS // BANK_BLOCKS):
-                bank = transpose_bank(nc, psum_t, identity[:], w_rows[m][:].bitcast(F32), h)
-                nc.scalar.copy(
-                    out=w_grouped_words[:, :, h * BANK_BLOCKS : (h + 1) * BANK_BLOCKS, :],
-                    in_=bank[:].rearrange("w c u p -> w p c u"),
-                )
+        for m in range(MASKS):
             nc.vector.quantize_mx(
                 out=w_codes[:, m, :].bitcast(E4M3_X4),
                 scales=w_scales[:, m, :],
-                in_=w_grouped[:],
+                in_=w_grouped[:, m * F * PACK : (m + 1) * F * PACK],
             )
 
         def mask_and_transpose(t):
             dz = masked.tile([P, ROW], BF16)
             nc.vector.scalar_tensor_tensor(
                 out=dz[:],
-                in0=z_tiles[t][:],
+                in0=z_tiles[t // Z_TILES][:, t % Z_TILES, :],
                 scalar=0.0,
                 in1=g_tiles[t // G_TILES][:, t % G_TILES, :],
                 op0=ALU.is_gt,
@@ -142,21 +137,20 @@ def tile_paralleldense_t_v_kernel(tc, x, W, b, z, grad_out, out):
                     start=True,
                     stop=True,
                 )
-                out_cols = out_sb[:, t % OUT_TILES, m * F : (m + 1) * F]
+                out_cols = out_sb[:, m * F : (m + 1) * F]
                 if m == VECTOR_MASK:
                     nc.vector.tensor_copy(out=out_cols, in_=acc[:])
                 else:
                     nc.scalar.copy(out=out_cols, in_=acc[:])
 
         grouped_next = mask_and_transpose(0)
-        for t in range(TILES):
-            grouped_now = grouped_next
-            if t + 1 < TILES:
-                grouped_next = mask_and_transpose(t + 1)
-            if t % OUT_TILES == 0:
-                out_sb = result.tile([P, OUT_TILES, ROW], F32)
-            quantise_and_multiply(t, grouped_now, out_sb)
-            if t % OUT_TILES == OUT_TILES - 1:
-                nc.sync.dma_start(
-                    out=out_view[:, t + 1 - OUT_TILES : t + 1, :], in_=out_sb[:]
-                )
+        first = 0
+        for n, tiles in enumerate(STORE_TILES):
+            out_sb = result.tile([P, tiles, ROW], F32, tag="store%d" % n)
+            for t in range(first, first + tiles):
+                grouped_now = grouped_next
+                if t + 1 < TILES:
+                    grouped_next = mask_and_transpose(t + 1)
+                quantise_and_multiply(t, grouped_now, out_sb[:, t - first, :])
+            nc.sync.dma_start(out=out_view[:, first : first + tiles, :], in_=out_sb[:])
+            first += tiles

@@ -20,8 +20,8 @@ W_ROWS = MASKS * F // P
 HALVES = 2
 WORDS = K // 2
 BANK_BLOCKS = 2
-G_TILES = 4
-Z_TILES = 2
+G_LOADS = (2, 2, 4)
+Z_LOADS = (1, 1, 2, 2, 2)
 STORE_TILES = (4, 2, 2)
 VECTOR_MASK = MASKS - 1
 
@@ -46,8 +46,8 @@ def tile_paralleldense_t_v_kernel(tc, x, W, b, z, grad_out, out):
     with ExitStack() as ctx:
         const = ctx.enter_context(tc.tile_pool(name="const", bufs=1))
         w_in = ctx.enter_context(tc.tile_pool(name="w_in", bufs=1))
-        g_in = ctx.enter_context(tc.tile_pool(name="g_in", bufs=TILES // G_TILES))
-        z_in = ctx.enter_context(tc.tile_pool(name="z_in", bufs=TILES // Z_TILES))
+        g_in = ctx.enter_context(tc.tile_pool(name="g_in", bufs=1))
+        z_in = ctx.enter_context(tc.tile_pool(name="z_in", bufs=1))
         result = ctx.enter_context(tc.tile_pool(name="result", bufs=1))
         masked = ctx.enter_context(tc.tile_pool(name="masked", bufs=2))
         regroup = ctx.enter_context(tc.tile_pool(name="regroup", bufs=3))
@@ -63,15 +63,17 @@ def tile_paralleldense_t_v_kernel(tc, x, W, b, z, grad_out, out):
         out_view = out.rearrange("(p t) m f -> p t (m f)", t=TILES)
         g_tiles = []
         z_tiles = []
-        for t in range(TILES):
-            if t % G_TILES == 0:
-                g_sb = g_in.tile([P, G_TILES, ROW], BF16)
-                nc.sync.dma_start(out=g_sb[:], in_=g_view[:, t : t + G_TILES, :])
-                g_tiles.append(g_sb)
-            if t % Z_TILES == 0:
-                z_sb = z_in.tile([P, Z_TILES, ROW], F32)
-                nc.sync.dma_start(out=z_sb[:], in_=z_view[:, t : t + Z_TILES, :])
-                z_tiles.append(z_sb)
+        g_starts = [sum(G_LOADS[:n]) for n in range(len(G_LOADS))]
+        for z_count in Z_LOADS:
+            t = len(z_tiles)
+            if t in g_starts:
+                g_count = G_LOADS[g_starts.index(t)]
+                g_sb = g_in.tile([P, g_count, ROW], BF16, tag="g%d" % t)
+                nc.sync.dma_start(out=g_sb[:], in_=g_view[:, t : t + g_count, :])
+                g_tiles.extend([g_sb[:, j, :] for j in range(g_count)])
+            z_sb = z_in.tile([P, z_count, ROW], F32, tag="z%d" % t)
+            nc.sync.dma_start(out=z_sb[:], in_=z_view[:, t : t + z_count, :])
+            z_tiles.extend([z_sb[:, j, :] for j in range(z_count)])
 
         identity = const.tile([P, P], F32)
         make_identity(nc, identity[:])
@@ -99,9 +101,9 @@ def tile_paralleldense_t_v_kernel(tc, x, W, b, z, grad_out, out):
             dz = masked.tile([P, ROW], BF16)
             nc.vector.scalar_tensor_tensor(
                 out=dz[:],
-                in0=z_tiles[t // Z_TILES][:, t % Z_TILES, :],
+                in0=z_tiles[t],
                 scalar=0.0,
-                in1=g_tiles[t // G_TILES][:, t % G_TILES, :],
+                in1=g_tiles[t],
                 op0=ALU.is_gt,
                 op1=ALU.mult,
             )

@@ -16,25 +16,26 @@ PACK = 4
 TOKENS, MASKS, K, F = 1024, 4, 512, 512
 TILES = TOKENS // P
 ROW = MASKS * K
-W_ROWS = MASKS * F // P
-HALVES = 2
+W_MASKS = 2
+W_ROWS = W_MASKS * F // P
+SQUARES = 2
 WORDS = K // 2
 BANK_BLOCKS = 2
 G_LOADS = (2, 2, 4)
-Z_LOADS = (1, 1, 2, 2, 2)
-STORE_TILES = (4, 2, 2)
-VECTOR_MASK = MASKS - 1
+Z_LOADS = (1, 1, 1, 1, 1, 1, 1, 1)
+STORES = (2, 2, 2, 1, 1)
+AHEAD = 2
+VECTOR_MASK = 0
 
 FLOPS = 2 * TOKENS * MASKS * K * F
 BYTES = 2 * MASKS * F * K + 4 * TOKENS * ROW + 2 * TOKENS * ROW + 4 * TOKENS * ROW
 
 
-def transpose_bank(nc, psum_t, identity, words, bank_index):
-    bank = psum_t.tile([P, BANK_BLOCKS, HALVES, P], F32)
-    first = bank_index * BANK_BLOCKS * WORDS
+def transpose_bank(nc, psum_t, identity, words):
+    bank = psum_t.tile([P, BANK_BLOCKS, SQUARES, P], F32)
     for b in range(BANK_BLOCKS):
-        for u in range(HALVES):
-            start = first + (b * HALVES + u) * P
+        for u in range(SQUARES):
+            start = b * WORDS + u * P
             nc.tensor.transpose(
                 out=bank[:, b, u, :], in_=words[:, start : start + P], identity=identity
             )
@@ -45,18 +46,24 @@ def tile_paralleldense_t_v_kernel(tc, x, W, b, z, grad_out, out):
     nc = tc.nc
     with ExitStack() as ctx:
         const = ctx.enter_context(tc.tile_pool(name="const", bufs=1))
-        w_in = ctx.enter_context(tc.tile_pool(name="w_in", bufs=1))
+        w_in = ctx.enter_context(tc.tile_pool(name="w_in", bufs=MASKS // W_MASKS))
         g_in = ctx.enter_context(tc.tile_pool(name="g_in", bufs=1))
         z_in = ctx.enter_context(tc.tile_pool(name="z_in", bufs=1))
         result = ctx.enter_context(tc.tile_pool(name="result", bufs=1))
-        masked = ctx.enter_context(tc.tile_pool(name="masked", bufs=2))
-        regroup = ctx.enter_context(tc.tile_pool(name="regroup", bufs=3))
+        masked = ctx.enter_context(tc.tile_pool(name="masked", bufs=3))
+        regroup = ctx.enter_context(tc.tile_pool(name="regroup", bufs=1))
         dz_mx = ctx.enter_context(tc.tile_pool(name="dz_mx", bufs=2))
         psum_t = ctx.enter_context(tc.psum_pool(name="psum_t", bufs=4))
         psum_o = ctx.enter_context(tc.psum_pool(name="psum_o", bufs=4))
 
-        w_sb = w_in.tile([P, W_ROWS * K], BF16)
-        nc.sync.dma_start(out=w_sb[:], in_=W.rearrange("m (q c) k -> (m q) (c k)", c=W_ROWS))
+        w_loads = []
+        for m in range(0, MASKS, W_MASKS):
+            w_sb = w_in.tile([P, W_ROWS * K], BF16)
+            nc.sync.dma_start(
+                out=w_sb[:],
+                in_=W[m : m + W_MASKS].rearrange("m (q c) k -> (m q) (c k)", c=W_ROWS),
+            )
+            w_loads.append(w_sb)
 
         g_view = grad_out.rearrange("(p t) c -> p t c", t=TILES)
         z_view = z.rearrange("(p t) m k -> p t (m k)", t=TILES)
@@ -80,24 +87,34 @@ def tile_paralleldense_t_v_kernel(tc, x, W, b, z, grad_out, out):
 
         w_codes = const.tile([P, MASKS, F], U32, align_bytes=64)
         w_scales = const.tile([P, MASKS, F], U8, align_bytes=64)
-        w_grouped = const.tile([P, MASKS * F * PACK], BF16, align_bytes=64)
-        w_grouped_words = (
-            w_grouped[:].bitcast(F32).rearrange("w (p c u) -> w p c u", c=W_ROWS, u=HALVES)
-        )
-        for h in range(W_ROWS // BANK_BLOCKS):
-            bank = transpose_bank(nc, psum_t, identity[:], w_sb[:].bitcast(F32), h)
-            nc.scalar.copy(
-                out=w_grouped_words[:, :, h * BANK_BLOCKS : (h + 1) * BANK_BLOCKS, :],
-                in_=bank[:].rearrange("w c u p -> w p c u"),
-            )
-        for m in range(MASKS):
-            nc.vector.quantize_mx(
-                out=w_codes[:, m, :].bitcast(E4M3_X4),
-                scales=w_scales[:, m, :],
-                in_=w_grouped[:, m * F * PACK : (m + 1) * F * PACK],
-            )
 
-        def mask_and_transpose(t):
+        def prepare_w(n):
+            w_grouped = regroup.tile([P, W_MASKS * F * PACK], BF16, tag="w%d" % n, align_bytes=64)
+            w_grouped_words = (
+                w_grouped[:].bitcast(F32).rearrange("w (p c u) -> w p c u", c=W_ROWS, u=SQUARES)
+            )
+            w_words = w_loads[n][:].bitcast(F32)
+            for c in range(0, W_ROWS, BANK_BLOCKS):
+                bank = transpose_bank(
+                    nc, psum_t, identity[:], w_words[:, c * WORDS : (c + BANK_BLOCKS) * WORDS]
+                )
+                nc.scalar.copy(
+                    out=w_grouped_words[:, :, c : c + BANK_BLOCKS, :],
+                    in_=bank[:].rearrange("w c u p -> w p c u"),
+                )
+            for j in range(W_MASKS):
+                m = n * W_MASKS + j
+                nc.vector.quantize_mx(
+                    out=w_codes[:, m, :].bitcast(E4M3_X4),
+                    scales=w_scales[:, m, :],
+                    in_=w_grouped[:, j * F * PACK : (j + 1) * F * PACK],
+                )
+
+        dz_tiles = {}
+        grouped = {}
+        products = {}
+
+        def mask(t):
             dz = masked.tile([P, ROW], BF16)
             nc.vector.scalar_tensor_tensor(
                 out=dz[:],
@@ -107,25 +124,31 @@ def tile_paralleldense_t_v_kernel(tc, x, W, b, z, grad_out, out):
                 op0=ALU.is_gt,
                 op1=ALU.mult,
             )
-            dz_grouped = regroup.tile([P, MASKS * P * PACK], BF16, tag="grouped", align_bytes=64)
-            dz_grouped_words = (
+            dz_tiles[t] = dz
+
+        def transpose_and_group(t):
+            dz_grouped = regroup.tile([P, ROW], BF16, tag="dz%d" % (t % 3), align_bytes=64)
+            words = dz_tiles[t][:].bitcast(F32)
+            grouped_words = (
                 dz_grouped[:]
                 .bitcast(F32)
-                .rearrange("w (m i u) -> w m i u", m=MASKS, u=HALVES)
+                .rearrange("w (m i u) -> w m i u", m=MASKS, u=SQUARES)
             )
-            for h in range(MASKS // BANK_BLOCKS):
-                bank = transpose_bank(nc, psum_t, identity[:], dz[:].bitcast(F32), h)
+            for m in range(0, MASKS, BANK_BLOCKS):
+                bank = transpose_bank(
+                    nc, psum_t, identity[:], words[:, m * WORDS : (m + BANK_BLOCKS) * WORDS]
+                )
                 nc.scalar.copy(
-                    out=dz_grouped_words[:, h * BANK_BLOCKS : (h + 1) * BANK_BLOCKS, :, :],
+                    out=grouped_words[:, m : m + BANK_BLOCKS, :, :],
                     in_=bank[:].rearrange("w m u i -> w m i u"),
                 )
-            return dz_grouped
+            grouped[t] = dz_grouped
 
-        def quantise_and_multiply(t, dz_grouped, out_sb):
+        def quantise_and_multiply(t):
             dz_codes = dz_mx.tile([P, MASKS * P], U32, align_bytes=64)
             dz_scales = dz_mx.tile([P, MASKS * P], U8, align_bytes=64)
             nc.vector.quantize_mx(
-                out=dz_codes[:].bitcast(E5M2_X4), scales=dz_scales[:], in_=dz_grouped[:]
+                out=dz_codes[:].bitcast(E5M2_X4), scales=dz_scales[:], in_=grouped[t][:]
             )
             for m in range(MASKS):
                 tokens = slice(m * P, (m + 1) * P)
@@ -139,20 +162,28 @@ def tile_paralleldense_t_v_kernel(tc, x, W, b, z, grad_out, out):
                     start=True,
                     stop=True,
                 )
-                out_cols = out_sb[:, m * F : (m + 1) * F]
-                if m == VECTOR_MASK:
-                    nc.vector.tensor_copy(out=out_cols, in_=acc[:])
-                else:
-                    nc.scalar.copy(out=out_cols, in_=acc[:])
+                products[t, m] = acc
 
-        grouped_next = mask_and_transpose(0)
-        first = 0
-        for n, tiles in enumerate(STORE_TILES):
-            out_sb = result.tile([P, tiles, ROW], F32, tag="store%d" % n)
-            for t in range(first, first + tiles):
-                grouped_now = grouped_next
-                if t + 1 < TILES:
-                    grouped_next = mask_and_transpose(t + 1)
-                quantise_and_multiply(t, grouped_now, out_sb[:, t - first, :])
-            nc.sync.dma_start(out=out_view[:, first : first + tiles, :], in_=out_sb[:])
-            first += tiles
+        def copy_out(t, m, out_row):
+            copy = nc.vector.tensor_copy if m == VECTOR_MASK and t % 2 == 1 else nc.scalar.copy
+            copy(out=out_row[:, m * F : (m + 1) * F], in_=products[t, m][:])
+
+        with tc.manual_schedule():
+            for n in range(MASKS // W_MASKS):
+                prepare_w(n)
+            for t in range(AHEAD):
+                mask(t)
+                transpose_and_group(t)
+            first = 0
+            for n, count in enumerate(STORES):
+                out_sb = result.tile([P, count, ROW], F32, tag="store%d" % n)
+                for t in range(first, first + count):
+                    quantise_and_multiply(t)
+                    if t + AHEAD < TILES:
+                        mask(t + AHEAD)
+                    for m in range(MASKS):
+                        copy_out(t, m, out_sb[:, t - first, :])
+                    if t + AHEAD < TILES:
+                        transpose_and_group(t + AHEAD)
+                nc.sync.dma_start(out=out_view[:, first : first + count, :], in_=out_sb[:])
+                first += count

@@ -21,9 +21,9 @@ W_ROWS = W_MASKS * F // P
 SQUARES = 2
 WORDS = K // 2
 BANK_BLOCKS = 2
-G_LOADS = (2, 2, 4)
-Z_LOADS = (1, 1, 1, 1, 1, 1, 1, 1)
-STORES = (2, 2, 2, 1, 1)
+G_LOADS = (4, 2, 2)
+Z_LOADS = (1, 1, 2, 2, 2)
+STORES = (2, 2, 2, 2)
 AHEAD = 2
 VECTOR_MASK = 0
 

@@ -16,16 +16,16 @@ PACK = 4
 TOKENS, MASKS, K, F = 1024, 4, 512, 512
 TILES = TOKENS // P
 ROW = MASKS * K
-W_MASKS = 2
+W_MASKS = 4
 W_ROWS = W_MASKS * F // P
 SQUARES = 2
 WORDS = K // 2
 BANK_BLOCKS = 2
 G_LOADS = (4, 2, 2)
-Z_LOADS = (1, 1, 2, 2, 2)
+Z_LOADS = (2, 2, 2, 2)
 STORES = (2, 2, 2, 2)
 AHEAD = 2
-VECTOR_MASK = 0
+VECTOR_EVEN, VECTOR_ODD, VECTOR_LAST = 0, 1, 2
 
 FLOPS = 2 * TOKENS * MASKS * K * F
 BYTES = 2 * MASKS * F * K + 4 * TOKENS * ROW + 2 * TOKENS * ROW + 4 * TOKENS * ROW
@@ -98,7 +98,8 @@ def tile_paralleldense_t_v_kernel(tc, x, W, b, z, grad_out, out):
                 bank = transpose_bank(
                     nc, psum_t, identity[:], w_words[:, c * WORDS : (c + BANK_BLOCKS) * WORDS]
                 )
-                nc.scalar.copy(
+                copy = nc.vector.tensor_copy if c // BANK_BLOCKS % 2 == 1 else nc.scalar.copy
+                copy(
                     out=w_grouped_words[:, :, c : c + BANK_BLOCKS, :],
                     in_=bank[:].rearrange("w c u p -> w p c u"),
                 )
@@ -116,14 +117,17 @@ def tile_paralleldense_t_v_kernel(tc, x, W, b, z, grad_out, out):
 
         def mask(t):
             dz = masked.tile([P, ROW], BF16)
-            nc.vector.scalar_tensor_tensor(
-                out=dz[:],
-                in0=z_tiles[t],
-                scalar=0.0,
-                in1=g_tiles[t],
-                op0=ALU.is_gt,
-                op1=ALU.mult,
-            )
+            pieces = 2 if t == 0 else 1
+            for j in range(pieces):
+                cols = slice(j * ROW // pieces, (j + 1) * ROW // pieces)
+                nc.vector.scalar_tensor_tensor(
+                    out=dz[:, cols],
+                    in0=z_tiles[t][:, cols],
+                    scalar=0.0,
+                    in1=g_tiles[t][:, cols],
+                    op0=ALU.is_gt,
+                    op1=ALU.mult,
+                )
             dz_tiles[t] = dz
 
         def transpose_and_group(t):
@@ -164,9 +168,14 @@ def tile_paralleldense_t_v_kernel(tc, x, W, b, z, grad_out, out):
                 )
                 products[t, m] = acc
 
-        def copy_out(t, m, out_row):
-            copy = nc.vector.tensor_copy if m == VECTOR_MASK and t % 2 == 1 else nc.scalar.copy
-            copy(out=out_row[:, m * F : (m + 1) * F], in_=products[t, m][:])
+        def copy_out(t, out_row):
+            if t + AHEAD >= TILES:
+                on_vector = VECTOR_LAST
+            else:
+                on_vector = VECTOR_ODD if t % 2 == 1 else VECTOR_EVEN
+            for m in range(MASKS):
+                copy = nc.vector.tensor_copy if m < on_vector else nc.scalar.copy
+                copy(out=out_row[:, m * F : (m + 1) * F], in_=products[t, m][:])
 
         with tc.manual_schedule():
             for n in range(MASKS // W_MASKS):
@@ -181,8 +190,7 @@ def tile_paralleldense_t_v_kernel(tc, x, W, b, z, grad_out, out):
                     quantise_and_multiply(t)
                     if t + AHEAD < TILES:
                         mask(t + AHEAD)
-                    for m in range(MASKS):
-                        copy_out(t, m, out_sb[:, t - first, :])
+                    copy_out(t, out_sb[:, t - first, :])
                     if t + AHEAD < TILES:
                         transpose_and_group(t + AHEAD)
                 nc.sync.dma_start(out=out_view[:, first : first + count, :], in_=out_sb[:])

@@ -23,7 +23,7 @@ WORDS = K // 2
 BANK_BLOCKS = 2
 G_LOADS = (4, 2, 2)
 Z_LOADS = (2, 2, 2, 2)
-STORES = (2, 2, 2, 2)
+STORES = (1, 1, 1, 1, 1, 1, 1, 1)
 AHEAD = 2
 VECTOR_EVEN, VECTOR_ODD, VECTOR_LAST = 0, 1, 2
 

@@ -58,7 +58,7 @@ def tile_paralleldense_t_v_kernel(tc, x, W, b, z, grad_out, out):
 
         w_loads = []
         for m in range(0, MASKS, W_MASKS):
-            w_sb = w_in.tile([P, W_ROWS * K], BF16)
+            w_sb = w_in.tile([P, W_ROWS * K], BF16, align_bytes=256)
             nc.sync.dma_start(
                 out=w_sb[:],
                 in_=W[m : m + W_MASKS].rearrange("m (q c) k -> (m q) (c k)", c=W_ROWS),
@@ -75,10 +75,10 @@ def tile_paralleldense_t_v_kernel(tc, x, W, b, z, grad_out, out):
             t = len(z_tiles)
             if t in g_starts:
                 g_count = G_LOADS[g_starts.index(t)]
-                g_sb = g_in.tile([P, g_count, ROW], BF16, tag="g%d" % t)
+                g_sb = g_in.tile([P, g_count, ROW], BF16, tag="g%d" % t, align_bytes=256)
                 nc.sync.dma_start(out=g_sb[:], in_=g_view[:, t : t + g_count, :])
                 g_tiles.extend([g_sb[:, j, :] for j in range(g_count)])
-            z_sb = z_in.tile([P, z_count, ROW], F32, tag="z%d" % t)
+            z_sb = z_in.tile([P, z_count, ROW], F32, tag="z%d" % t, align_bytes=256)
             nc.sync.dma_start(out=z_sb[:], in_=z_view[:, t : t + z_count, :])
             z_tiles.extend([z_sb[:, j, :] for j in range(z_count)])
 
@@ -185,7 +185,7 @@ def tile_paralleldense_t_v_kernel(tc, x, W, b, z, grad_out, out):
                 transpose_and_group(t)
             first = 0
             for n, count in enumerate(STORES):
-                out_sb = result.tile([P, count, ROW], F32, tag="store%d" % n)
+                out_sb = result.tile([P, count, ROW], F32, tag="store%d" % n, align_bytes=256)
                 for t in range(first, first + count):
                     quantise_and_multiply(t)
                     if t + AHEAD < TILES:

from contextlib import ExitStack

import concourse.mybir as mybir
from concourse.masks import make_identity

F32 = mybir.dt.float32
BF16 = mybir.dt.bfloat16
U32 = mybir.dt.uint32
U8 = mybir.dt.uint8
E5M2_X4 = mybir.dt.float8_e5m2_x4
E4M3_X4 = mybir.dt.float8_e4m3fn_x4
ALU = mybir.AluOpType

P = 128
PACK = 4
TOKENS, MASKS, K, F = 1024, 4, 512, 512
TILES = TOKENS // P
ROW = MASKS * K
W_MASKS = 4
W_ROWS = W_MASKS * F // P
SQUARES = 2
WORDS = K // 2
BANK_BLOCKS = 2
G_LOADS = (4, 2, 2)
Z_LOADS = (2, 2, 2, 2)
STORES = (1, 1, 1, 1, 1, 1, 1, 1)
AHEAD = 2
VECTOR_EVEN, VECTOR_ODD, VECTOR_LAST = 0, 1, 2

FLOPS = 2 * TOKENS * MASKS * K * F
BYTES = 2 * MASKS * F * K + 4 * TOKENS * ROW + 2 * TOKENS * ROW + 4 * TOKENS * ROW


def transpose_bank(nc, psum_t, identity, words):
    bank = psum_t.tile([P, BANK_BLOCKS, SQUARES, P], F32)
    for b in range(BANK_BLOCKS):
        for u in range(SQUARES):
            start = b * WORDS + u * P
            nc.tensor.transpose(
                out=bank[:, b, u, :], in_=words[:, start : start + P], identity=identity
            )
    return bank


def tile_paralleldense_t_v_kernel(tc, x, W, b, z, grad_out, out):
    nc = tc.nc
    with ExitStack() as ctx:
        const = ctx.enter_context(tc.tile_pool(name="const", bufs=1))
        w_in = ctx.enter_context(tc.tile_pool(name="w_in", bufs=MASKS // W_MASKS))
        g_in = ctx.enter_context(tc.tile_pool(name="g_in", bufs=1))
        z_in = ctx.enter_context(tc.tile_pool(name="z_in", bufs=1))
        result = ctx.enter_context(tc.tile_pool(name="result", bufs=1))
        masked = ctx.enter_context(tc.tile_pool(name="masked", bufs=3))
        regroup = ctx.enter_context(tc.tile_pool(name="regroup", bufs=1))
        dz_mx = ctx.enter_context(tc.tile_pool(name="dz_mx", bufs=2))
        psum_t = ctx.enter_context(tc.psum_pool(name="psum_t", bufs=4))
        psum_o = ctx.enter_context(tc.psum_pool(name="psum_o", bufs=4))

        w_loads = []
        for m in range(0, MASKS, W_MASKS):
            w_sb = w_in.tile([P, W_ROWS * K], BF16, align_bytes=256)
            nc.sync.dma_start(
                out=w_sb[:],
                in_=W[m : m + W_MASKS].rearrange("m (q c) k -> (m q) (c k)", c=W_ROWS),
            )
            w_loads.append(w_sb)

        g_view = grad_out.rearrange("(p t) c -> p t c", t=TILES)
        z_view = z.rearrange("(p t) m k -> p t (m k)", t=TILES)
        out_view = out.rearrange("(p t) m f -> p t (m f)", t=TILES)
        g_tiles = []
        z_tiles = []
        g_starts = [sum(G_LOADS[:n]) for n in range(len(G_LOADS))]
        for z_count in Z_LOADS:
            t = len(z_tiles)
            if t in g_starts:
                g_count = G_LOADS[g_starts.index(t)]
                g_sb = g_in.tile([P, g_count, ROW], BF16, tag="g%d" % t, align_bytes=256)
                nc.sync.dma_start(out=g_sb[:], in_=g_view[:, t : t + g_count, :])
                g_tiles.extend([g_sb[:, j, :] for j in range(g_count)])
            z_sb = z_in.tile([P, z_count, ROW], F32, tag="z%d" % t, align_bytes=256)
            nc.sync.dma_start(out=z_sb[:], in_=z_view[:, t : t + z_count, :])
            z_tiles.extend([z_sb[:, j, :] for j in range(z_count)])

        identity = const.tile([P, P], F32)
        make_identity(nc, identity[:])

        w_codes = const.tile([P, MASKS, F], U32, align_bytes=64)
        w_scales = const.tile([P, MASKS, F], U8, align_bytes=64)

        def prepare_w(n):
            w_grouped = regroup.tile([P, W_MASKS * F * PACK], BF16, tag="w%d" % n, align_bytes=64)
            w_grouped_words = (
                w_grouped[:].bitcast(F32).rearrange("w (p c u) -> w p c u", c=W_ROWS, u=SQUARES)
            )
            w_words = w_loads[n][:].bitcast(F32)
            for c in range(0, W_ROWS, BANK_BLOCKS):
                bank = transpose_bank(
                    nc, psum_t, identity[:], w_words[:, c * WORDS : (c + BANK_BLOCKS) * WORDS]
                )
                copy = nc.vector.tensor_copy if c // BANK_BLOCKS % 2 == 1 else nc.scalar.copy
                copy(
                    out=w_grouped_words[:, :, c : c + BANK_BLOCKS, :],
                    in_=bank[:].rearrange("w c u p -> w p c u"),
                )
            for j in range(W_MASKS):
                m = n * W_MASKS + j
                nc.vector.quantize_mx(
                    out=w_codes[:, m, :].bitcast(E4M3_X4),
                    scales=w_scales[:, m, :],
                    in_=w_grouped[:, j * F * PACK : (j + 1) * F * PACK],
                )

        dz_tiles = {}
        grouped = {}
        products = {}

        def mask(t):
            dz = masked.tile([P, ROW], BF16)
            pieces = 2 if t == 0 else 1
            for j in range(pieces):
                cols = slice(j * ROW // pieces, (j + 1) * ROW // pieces)
                nc.vector.scalar_tensor_tensor(
                    out=dz[:, cols],
                    in0=z_tiles[t][:, cols],
                    scalar=0.0,
                    in1=g_tiles[t][:, cols],
                    op0=ALU.is_gt,
                    op1=ALU.mult,
                )
            dz_tiles[t] = dz

        def transpose_and_group(t):
            dz_grouped = regroup.tile([P, ROW], BF16, tag="dz%d" % (t % 3), align_bytes=64)
            words = dz_tiles[t][:].bitcast(F32)
            grouped_words = (
                dz_grouped[:]
                .bitcast(F32)
                .rearrange("w (m i u) -> w m i u", m=MASKS, u=SQUARES)
            )
            for m in range(0, MASKS, BANK_BLOCKS):
                bank = transpose_bank(
                    nc, psum_t, identity[:], words[:, m * WORDS : (m + BANK_BLOCKS) * WORDS]
                )
                nc.scalar.copy(
                    out=grouped_words[:, m : m + BANK_BLOCKS, :, :],
                    in_=bank[:].rearrange("w m u i -> w m i u"),
                )
            grouped[t] = dz_grouped

        def quantise_and_multiply(t):
            dz_codes = dz_mx.tile([P, MASKS * P], U32, align_bytes=64)
            dz_scales = dz_mx.tile([P, MASKS * P], U8, align_bytes=64)
            nc.vector.quantize_mx(
                out=dz_codes[:].bitcast(E5M2_X4), scales=dz_scales[:], in_=grouped[t][:]
            )
            for m in range(MASKS):
                tokens = slice(m * P, (m + 1) * P)
                acc = psum_o.tile([P, F], F32)
                nc.tensor.matmul_mx(
                    out=acc[:],
                    lhsT=dz_codes[:, tokens].bitcast(E5M2_X4),
                    lhsT_scale=dz_scales[:, tokens],
                    rhs=w_codes[:, m, :].bitcast(E4M3_X4),
                    rhs_scale=w_scales[:, m, :],
                    start=True,
                    stop=True,
                )
                products[t, m] = acc

        def copy_out(t, out_row):
            if t + AHEAD >= TILES:
                on_vector = VECTOR_LAST
            else:
                on_vector = VECTOR_ODD if t % 2 == 1 else VECTOR_EVEN
            for m in range(MASKS):
                copy = nc.vector.tensor_copy if m < on_vector else nc.scalar.copy
                copy(out=out_row[:, m * F : (m + 1) * F], in_=products[t, m][:])

        with tc.manual_schedule():
            for n in range(MASKS // W_MASKS):
                prepare_w(n)
            for t in range(AHEAD):
                mask(t)
                transpose_and_group(t)
            first = 0
            for n, count in enumerate(STORES):
                out_sb = result.tile([P, count, ROW], F32, tag="store%d" % n, align_bytes=256)
                for t in range(first, first + count):
                    quantise_and_multiply(t)
                    if t + AHEAD < TILES:
                        mask(t + AHEAD)
                    copy_out(t, out_sb[:, t - first, :])
                    if t + AHEAD < TILES:
                        transpose_and_group(t + AHEAD)
                nc.sync.dma_start(out=out_view[:, first : first + count, :], in_=out_sb[:])
                first += count
